import numpy as np
import ml_dtypes


def mxq(x, axis, fmt="e4m3"):
    dtype, down = {"e4m3": (ml_dtypes.float8_e4m3fn, 7), "e5m2": (ml_dtypes.float8_e5m2, 14)}[fmt]
    v = np.moveaxis(np.asarray(x, np.float32).astype(ml_dtypes.bfloat16).astype(np.float64), axis, -1)
    blocks = v.reshape(v.shape[:-1] + (-1, 32))
    amax = np.abs(blocks).max(-1, keepdims=True)
    byte = np.maximum(np.where(amax > 0, np.frexp(amax)[1] - 1 + 127, 0) - down, 1)
    scale = np.exp2(byte - 127.0)
    codes = (blocks / scale).astype(np.float32).astype(dtype).astype(np.float64)
    return np.moveaxis((codes * scale).reshape(v.shape), -1, axis)


WIDE = False


def mx_kscale(k):
    if not WIDE:
        return np.ones(k)
    levels = np.array([10, -10, 5, -5, 0])
    a = np.random.permutation(np.resize(levels, k // 512 * 4)).reshape(k // 512, 4)
    idx = np.arange(k)
    return np.exp2(a[idx // 512, idx % 128 // 32])


BF16 = ml_dtypes.bfloat16


def bf(x):
    return np.asarray(x, np.float32).astype(BF16)


def f64(x):
    return np.asarray(x).astype(np.float64)


B, N, D, H = 512, 17, 1024, 32
D2 = D // 2
D4 = D // 4
EPS = 1e-5


def layernorm(z, g, b):
    mu = z.mean(-1, keepdims=True)
    var = z.var(-1, keepdims=True)
    return (z - mu) / np.sqrt(var + EPS) * g + b


def setup_inputs():
    s, t = mx_kscale(D), mx_kscale(D2)
    r = np.random.standard_normal
    return {"query": bf(r((B, N, D)) * s),
            "A1W": bf(r((D, D2)) / np.sqrt(D) / s[:, None]),
            "A1b": bf(r(D2) * 0.2),
            "g1": bf((1.0 + 0.1 * r(D2)) * t),
            "b1": bf(r(D2) * 0.2 * t),
            "A2W": bf(r((D2, D4)) / np.sqrt(D2) / t[:, None]),
            "A2b": bf(r(D4) * 0.2),
            "g2": bf(1.0 + 0.1 * r(D4)),
            "b2": bf(r(D4) * 0.2)}


def reference(query, A1W, A1b, g1, b1, A2W, A2b, g2, b2):
    u = (mxq(f64(query), 2, "e4m3") @ mxq(f64(A1W), 0, "e4m3")) + f64(A1b)
    j1 = np.maximum(layernorm(u, f64(g1), f64(b1)), 0.0)
    w = (mxq(j1, 2, "e4m3") @ mxq(f64(A2W), 0, "e4m3")) + f64(A2b)
    return np.maximum(layernorm(w, f64(g2), f64(b2)), 0.0)

@@ -1,0 +1,357 @@
+from contextlib import ExitStack
+
+import concourse.mybir as mybir
+from concourse.masks import make_identity
+
+F32 = mybir.dt.float32
+BF16 = mybir.dt.bfloat16
+U32 = mybir.dt.uint32
+U8 = mybir.dt.uint8
+FP8X4 = mybir.dt.float8_e4m3fn_x4
+ALU = mybir.AluOpType
+ACT = mybir.ActivationFunctionType
+
+P = 128
+PACK = 4
+ROWS = 512 * 17
+D = 1024
+D2 = 512
+D4 = 256
+EPS = 1e-5
+TILES = 4
+BLOCK = TILES * P
+BLOCKS = ROWS // BLOCK
+PASSES = D // (P * PACK)
+
+FLOPS = 2 * ROWS * (D * D2 + D2 * D4)
+
+Q_COPY = 0
+LOAD = 3
+Q_QUANTISE = 4
+U_BIAS = 6
+U_STATS = 10
+U_NORMALISE = 11
+J1_PLANE = 16
+J1_GROUP = 21
+J1_QUANTISE = 22
+W_BIAS = 24
+W_STATS = 28
+W_AFFINE = 29
+O_STORE = 33
+
+
+def quantise_weight(nc, pool, raw, codes, scales, width):
+    grouped = pool.tile([P, width, PACK], BF16, align_bytes=64, name="grouped", tag="grouped%d" % width)
+    nc.vector.tensor_copy(out=grouped[:], in_=raw.rearrange("p t n -> p n t"))
+    nc.vector.quantize_mx(
+        out=codes.bitcast(FP8X4), scales=scales, in_=grouped[:].rearrange("p n t -> p (n t)")
+    )
+
+
+def tile_multiheadedattention_pa_t_kernel(tc, query, A1W, A1b, g1, b1, A2W, A2b, g2, b2, out):
+    nc = tc.nc
+    q_rows = query.flatten_outer_dims()
+    out_rows = out.flatten_outer_dims()
+
+    with ExitStack() as ctx:
+        const = ctx.enter_context(tc.tile_pool(name="const", bufs=1))
+        two = ctx.enter_context(tc.tile_pool(name="two", bufs=2))
+        three = ctx.enter_context(tc.tile_pool(name="three", bufs=3))
+        small = ctx.enter_context(tc.tile_pool(name="small", bufs=4))
+        psum = ctx.enter_context(tc.psum_pool(name="psum", bufs=2))
+
+        held = {}
+
+        def block_rows(b):
+            return slice(b * BLOCK, (b + 1) * BLOCK)
+
+        def load(b):
+            q_sb = three.tile([P, TILES * D], BF16, name="q_sb")
+            nc.sync.dma_start(out=q_sb[:], in_=q_rows[block_rows(b), :].rearrange("(p j) k -> p (j k)", j=TILES))
+            held["q_sb", b] = q_sb
+
+        def q_transpose(b, j):
+            q_words = held["q_sb", b][:].bitcast(F32)
+            qT = psum.tile([P, D2], F32, name="qT")
+            for h in range(D2 // P):
+                col = j * D2 + h * P
+                nc.tensor.transpose(qT[:, h * P : (h + 1) * P], q_words[:, col : col + P], ident[:])
+            held["qT", b, j] = qT
+
+        def q_copy(b, j):
+            if j == 0:
+                held["qg", b] = two.tile([P, TILES * D], BF16, align_bytes=64, name="qg")
+            qg_words = held["qg", b][:].bitcast(F32)
+            nc.scalar.copy(
+                out=qg_words[:, j * D2 : (j + 1) * D2].rearrange("p (g r u) -> p g r u", g=PASSES, u=2),
+                in_=held["qT", b, j][:].rearrange("p (g u r) -> p g r u", g=PASSES, u=2),
+            )
+
+        def q_quantise(b):
+            q_codes = two.tile([P, TILES * PASSES * P], U32, align_bytes=64, name="q_codes")
+            q_scales = two.tile([P, TILES * PASSES * P], U8, align_bytes=64, name="q_scales")
+            nc.vector.quantize_mx(out=q_codes[:].bitcast(FP8X4), scales=q_scales[:], in_=held["qg", b][:])
+            held["q_codes", b] = q_codes
+            held["q_scales", b] = q_scales
+
+        def u_matmul(b, j):
+            mm1 = psum.tile([P, D2], F32, name="mm1")
+            for g in range(PASSES):
+                cols = slice((j * PASSES + g) * P, (j * PASSES + g + 1) * P)
+                nc.tensor.matmul_mx(
+                    out=mm1[:],
+                    lhsT=held["q_codes", b][:, cols].bitcast(FP8X4),
+                    lhsT_scale=held["q_scales", b][:, cols],
+                    rhs=a1_codes[:, g, :].bitcast(FP8X4),
+                    rhs_scale=a1_scales[:, g, :],
+                    start=(g == 0),
+                    stop=(g == PASSES - 1),
+                )
+            held["mm1", b, j] = mm1
+
+        def u_bias(b, j):
+            if j == 0:
+                held["u", b] = three.tile([P, TILES, D2], F32, name="u_sb")
+                held["u_sum", b] = small.tile([P, TILES], F32, name="u_sum")
+            nc.vector.scalar_tensor_tensor(
+                out=held["u", b][:, j, :],
+                in0=held["mm1", b, j][:],
+                scalar=1.0,
+                in1=a1b_all[:],
+                op0=ALU.mult,
+                op1=ALU.add,
+                accum_out=held["u_sum", b][:, j : j + 1],
+            )
+
+        def u_squares(b, j):
+            if j == 0:
+                held["u_sq", b] = two.tile([P, TILES, D2], BF16, name="u_sq")
+                held["u_ssq", b] = small.tile([P, TILES], F32, name="u_ssq")
+            nc.scalar.activation(
+                out=held["u_sq", b][:, j, :],
+                in_=held["u", b][:, j, :],
+                func=ACT.Square,
+                bias=held["u_sum", b][:, j : j + 1],
+                scale=-1.0 * D2,
+                accum_out=held["u_ssq", b][:, j : j + 1],
+            )
+
+        def u_stats(b):
+            u_std = small.tile([P, TILES], F32, name="u_std")
+            nc.scalar.activation(
+                out=u_std[:], in_=held["u_ssq", b][:], func=ACT.Sqrt, bias=eps[:, 0:1], scale=1.0 / (D2 * D2 * D2)
+            )
+            u_negmean = small.tile([P, TILES], F32, name="u_negmean")
+            nc.gpsimd.tensor_scalar(
+                out=u_negmean[:], in0=held["u_sum", b][:], scalar1=-1.0 / D2, scalar2=0.0, op0=ALU.mult, op1=ALU.add
+            )
+            held["u_std", b] = u_std
+            held["u_negmean", b] = u_negmean
+
+        def u_normalise(b, j):
+            if j == 0:
+                held["u_rstd", b] = small.tile([P, TILES], F32, name="u_rstd")
+                nc.vector.reciprocal(out=held["u_rstd", b][:], in_=held["u_std", b][:])
+                held["y", b] = two.tile([P, TILES, D2], F32, name="y_sb")
+            nc.vector.tensor_scalar(
+                out=held["y", b][:, j, :],
+                in0=held["u", b][:, j, :],
+                scalar1=held["u_negmean", b][:, j : j + 1],
+                scalar2=held["u_rstd", b][:, j : j + 1],
+                op0=ALU.add,
+                op1=ALU.mult,
+            )
+
+        def y_transpose(b, t):
+            yT = psum.tile([P, BLOCK], F32, name="yT")
+            for j in range(TILES):
+                nc.tensor.transpose(yT[:, j * P : (j + 1) * P], held["y", b][:, j, t * P : (t + 1) * P], ident[:])
+            held["yT", b, t] = yT
+
+        def j1_plane(b, t):
+            if t == 0:
+                held["j1_planes", b] = two.tile([P, PACK, BLOCK], BF16, name="j1_planes")
+            nc.scalar.activation(
+                out=held["j1_planes", b][:, t, :],
+                in_=held["yT", b, t][:],
+                func=ACT.Relu,
+                bias=gb_cols[:, PACK + t : PACK + t + 1],
+                scale=gb_cols[:, t : t + 1],
+            )
+
+        def j1_group(b):
+            j1_grouped = two.tile([P, BLOCK, PACK], BF16, align_bytes=64, name="j1_grouped")
+            nc.vector.tensor_copy(
+                out=j1_grouped[:].rearrange("p (c i) t -> p c t i", i=4),
+                in_=held["j1_planes", b][:].rearrange("p t (c i) -> p c t i", i=4),
+            )
+            held["j1_grouped", b] = j1_grouped
+
+        def j1_quantise(b):
+            j1_codes = two.tile([P, BLOCK], U32, align_bytes=64, name="j1_codes")
+            j1_scales = two.tile([P, BLOCK], U8, align_bytes=64, name="j1_scales")
+            nc.vector.quantize_mx(
+                out=j1_codes[:].bitcast(FP8X4),
+                scales=j1_scales[:],
+                in_=held["j1_grouped", b][:].rearrange("p r t -> p (r t)"),
+            )
+            held["j1_codes", b] = j1_codes
+            held["j1_scales", b] = j1_scales
+
+        def w_matmul(b, j):
+            mm2 = psum.tile([P, D4], F32, name="mm2")
+            nc.tensor.matmul_mx(
+                out=mm2[:],
+                lhsT=held["j1_codes", b][:, j * P : (j + 1) * P].bitcast(FP8X4),
+                lhsT_scale=held["j1_scales", b][:, j * P : (j + 1) * P],
+                rhs=a2_codes[:].bitcast(FP8X4),
+                rhs_scale=a2_scales[:],
+                start=True,
+                stop=True,
+            )
+            held["mm2", b, j] = mm2
+
+        def w_bias(b, j):
+            if j == 0:
+                held["w", b] = three.tile([P, TILES, D4], F32, name="w_sb")
+                held["w_sum", b] = small.tile([P, TILES], F32, name="w_sum")
+            nc.vector.scalar_tensor_tensor(
+                out=held["w", b][:, j, :],
+                in0=held["mm2", b, j][:],
+                scalar=1.0,
+                in1=a2b_all[:],
+                op0=ALU.mult,
+                op1=ALU.add,
+                accum_out=held["w_sum", b][:, j : j + 1],
+            )
+
+        def w_squares(b, j):
+            if j == 0:
+                held["w_sq", b] = two.tile([P, TILES, D4], BF16, name="w_sq")
+                held["w_ssq", b] = small.tile([P, TILES], F32, name="w_ssq")
+            nc.scalar.activation(
+                out=held["w_sq", b][:, j, :],
+                in_=held["w", b][:, j, :],
+                func=ACT.Square,
+                bias=held["w_sum", b][:, j : j + 1],
+                scale=-1.0 * D4,
+                accum_out=held["w_ssq", b][:, j : j + 1],
+            )
+
+        def w_stats(b):
+            w_std = small.tile([P, TILES], F32, name="w_std")
+            nc.scalar.activation(
+                out=w_std[:], in_=held["w_ssq", b][:], func=ACT.Sqrt, bias=eps[:, 0:1], scale=1.0 / (D4 * D4 * D4)
+            )
+            w_negmean = small.tile([P, TILES], F32, name="w_negmean")
+            nc.gpsimd.tensor_scalar(
+                out=w_negmean[:], in0=held["w_sum", b][:], scalar1=-1.0 / D4, scalar2=0.0, op0=ALU.mult, op1=ALU.add
+            )
+            held["w_std", b] = w_std
+            held["w_negmean", b] = w_negmean
+
+        def w_affine(b, j):
+            if j == 0:
+                held["w_rstd", b] = small.tile([P, TILES], F32, name="w_rstd")
+                nc.vector.reciprocal(out=held["w_rstd", b][:], in_=held["w_std", b][:])
+                held["w_gain", b] = two.tile([P, TILES, D4], F32, name="w_gain")
+                held["o", b] = three.tile([P, TILES, D4], F32, name="o_sb")
+            nc.vector.scalar_tensor_tensor(
+                out=held["w_gain", b][:, j, :],
+                in0=held["w", b][:, j, :],
+                scalar=held["w_negmean", b][:, j : j + 1],
+                in1=g2_all[:],
+                op0=ALU.add,
+                op1=ALU.mult,
+            )
+            nc.vector.scalar_tensor_tensor(
+                out=held["o", b][:, j, :],
+                in0=held["w_gain", b][:, j, :],
+                scalar=held["w_rstd", b][:, j : j + 1],
+                in1=b2_all[:],
+                op0=ALU.mult,
+                op1=ALU.add,
+            )
+
+        def o_store(b):
+            o_sb = held["o", b]
+            nc.scalar.activation(out=o_sb[:], in_=o_sb[:], func=ACT.Relu)
+            nc.sync.dma_start(out=out_rows[block_rows(b), :].rearrange("(p j) n -> p j n", j=TILES), in_=o_sb[:])
+
+        load(0)
+        ident = const.tile([P, P], F32)
+        make_identity(nc, ident[:])
+        eps = const.tile([P, 1], F32)
+        nc.vector.memset(eps[:], EPS)
+
+        a1_raw = const.tile([P, PASSES * PACK, D2], BF16)
+        nc.scalar.dma_start(
+            out=a1_raw[:].rearrange("p (h e) n -> p h (e n)", e=2),
+            in_=A1W.rearrange("(h p e) n -> p h (e n)", p=P, e=2),
+        )
+        a1_codes = const.tile([P, PASSES, D2], U32, align_bytes=64)
+        a1_scales = const.tile([P, PASSES, D2], U8, align_bytes=64)
+        for g in range(PASSES):
+            quantise_weight(
+                nc, const, a1_raw[:, g * PACK : (g + 1) * PACK, :], a1_codes[:, g, :], a1_scales[:, g, :], D2
+            )
+
+        a1b_all = const.tile([P, D2], BF16)
+        nc.scalar.dma_start(out=a1b_all[:], in_=A1b.partition_broadcast(P))
+
+        gb_rows = const.tile([P, P], BF16)
+        nc.vector.memset(gb_rows[:], 0.0)
+        nc.scalar.dma_start(out=gb_rows[0:PACK, :], in_=g1.rearrange("(t p) -> t p", p=P))
+        nc.scalar.dma_start(out=gb_rows[PACK : 2 * PACK, :], in_=b1.rearrange("(t p) -> t p", p=P))
+        gb_f32 = const.tile([P, P], F32)
+        nc.vector.tensor_copy(out=gb_f32[:], in_=gb_rows[:])
+        gb_ps = psum.tile([P, BLOCK], F32, name="yT")
+        nc.tensor.transpose(gb_ps[:, 0:P], gb_f32[:], ident[:])
+        gb_cols = const.tile([P, 2 * PACK], F32)
+        nc.vector.tensor_copy(out=gb_cols[:], in_=gb_ps[:, 0 : 2 * PACK])
+
+        a2_raw = const.tile([P, PACK, D4], BF16)
+        nc.scalar.dma_start(out=a2_raw[:], in_=A2W.rearrange("(t p) n -> p t n", p=P))
+        a2_codes = const.tile([P, D4], U32, align_bytes=64)
+        a2_scales = const.tile([P, D4], U8, align_bytes=64)
+        quantise_weight(nc, const, a2_raw[:], a2_codes[:], a2_scales[:], D4)
+        a2b_all = const.tile([P, D4], BF16)
+        nc.scalar.dma_start(out=a2b_all[:], in_=A2b.partition_broadcast(P))
+        g2_all = const.tile([P, D4], BF16)
+        nc.scalar.dma_start(out=g2_all[:], in_=g2.partition_broadcast(P))
+        b2_all = const.tile([P, D4], BF16)
+        nc.scalar.dma_start(out=b2_all[:], in_=b2.partition_broadcast(P))
+
+        load(1)
+        load(2)
+
+        def for_tile(stage, n):
+            if 0 <= n < BLOCKS * TILES:
+                stage(n // TILES, n % TILES)
+
+        def for_block(stage, n, ahead=0):
+            if n % TILES == 0 and 0 <= n // TILES + ahead < BLOCKS and n >= 0:
+                stage(n // TILES + ahead)
+
+        with tc.manual_schedule():
+            for step in range(-1, BLOCKS * TILES + O_STORE + 1):
+                for_tile(q_transpose, step + 1 - Q_COPY)
+                for_tile(u_matmul, step + 1 - U_BIAS)
+                for_tile(y_transpose, step + 1 - J1_PLANE)
+                for_tile(w_matmul, step + 1 - W_BIAS)
+
+                for_tile(u_bias, step - U_BIAS)
+                for_tile(q_copy, step - Q_COPY)
+                for_tile(u_normalise, step - U_NORMALISE)
+                for_tile(j1_plane, step - J1_PLANE)
+                for_tile(w_bias, step - W_BIAS)
+                for_tile(u_squares, step - U_BIAS)
+                for_block(u_stats, step - U_STATS)
+                for_tile(w_affine, step - W_AFFINE)
+                for_tile(w_squares, step - W_BIAS)
+                for_block(w_stats, step - W_STATS)
+                for_block(q_quantise, step - Q_QUANTISE)
+                for_block(j1_group, step - J1_GROUP)
+                for_block(j1_quantise, step - J1_QUANTISE)
+                for_block(o_store, step - O_STORE)
+                for_block(load, step - LOAD, ahead=3)

@@ -30,14 +30,17 @@ LOAD = 3
 Q_QUANTISE = 4
 U_BIAS = 6
 U_STATS = 10
-U_NORMALISE = 11
-J1_PLANE = 16
-J1_GROUP = 21
-J1_QUANTISE = 22
-W_BIAS = 24
-W_STATS = 28
-W_AFFINE = 29
-O_STORE = 33
+U_RSTD = 11
+U_NORMALISE = 12
+J1_PLANE = 17
+J1_GROUP = 22
+J1_QUANTISE = 23
+W_BIAS = 25
+W_STATS = 29
+W_RSTD = 30
+W_GAIN = 30
+W_SHIFT = 31
+O_STORE = 35
 
 
 def quantise_weight(nc, pool, raw, codes, scales, width):
@@ -148,10 +151,12 @@ def tile_multiheadedattention_pa_t_kernel(tc, query, A1W, A1b, g1, b1, A2W, A2b,
             held["u_std", b] = u_std
             held["u_negmean", b] = u_negmean
 
+        def u_rstd(b):
+            held["u_rstd", b] = small.tile([P, TILES], F32, name="u_rstd")
+            nc.vector.reciprocal(out=held["u_rstd", b][:], in_=held["u_std", b][:])
+
         def u_normalise(b, j):
             if j == 0:
-                held["u_rstd", b] = small.tile([P, TILES], F32, name="u_rstd")
-                nc.vector.reciprocal(out=held["u_rstd", b][:], in_=held["u_std", b][:])
                 held["y", b] = two.tile([P, TILES, D2], F32, name="y_sb")
             nc.vector.tensor_scalar(
                 out=held["y", b][:, j, :],
@@ -250,12 +255,13 @@ def tile_multiheadedattention_pa_t_kernel(tc, query, A1W, A1b, g1, b1, A2W, A2b,
             held["w_std", b] = w_std
             held["w_negmean", b] = w_negmean
 
-        def w_affine(b, j):
+        def w_rstd(b):
+            held["w_rstd", b] = small.tile([P, TILES], F32, name="w_rstd")
+            nc.vector.reciprocal(out=held["w_rstd", b][:], in_=held["w_std", b][:])
+
+        def w_gain(b, j):
             if j == 0:
-                held["w_rstd", b] = small.tile([P, TILES], F32, name="w_rstd")
-                nc.vector.reciprocal(out=held["w_rstd", b][:], in_=held["w_std", b][:])
                 held["w_gain", b] = two.tile([P, TILES, D4], F32, name="w_gain")
-                held["o", b] = three.tile([P, TILES, D4], F32, name="o_sb")
             nc.vector.scalar_tensor_tensor(
                 out=held["w_gain", b][:, j, :],
                 in0=held["w", b][:, j, :],
@@ -264,6 +270,10 @@ def tile_multiheadedattention_pa_t_kernel(tc, query, A1W, A1b, g1, b1, A2W, A2b,
                 op0=ALU.add,
                 op1=ALU.mult,
             )
+
+        def w_shift(b, j):
+            if j == 0:
+                held["o", b] = three.tile([P, TILES, D4], F32, name="o_sb")
             nc.vector.scalar_tensor_tensor(
                 out=held["o", b][:, j, :],
                 in0=held["w_gain", b][:, j, :],
@@ -336,8 +346,8 @@ def tile_multiheadedattention_pa_t_kernel(tc, query, A1W, A1b, g1, b1, A2W, A2b,
         with tc.manual_schedule():
             for step in range(-1, BLOCKS * TILES + O_STORE + 1):
                 for_tile(q_transpose, step + 1 - Q_COPY)
-                for_tile(u_matmul, step + 1 - U_BIAS)
                 for_tile(y_transpose, step + 1 - J1_PLANE)
+                for_tile(u_matmul, step + 1 - U_BIAS)
                 for_tile(w_matmul, step + 1 - W_BIAS)
 
                 for_tile(u_bias, step - U_BIAS)
@@ -347,11 +357,14 @@ def tile_multiheadedattention_pa_t_kernel(tc, query, A1W, A1b, g1, b1, A2W, A2b,
                 for_tile(w_bias, step - W_BIAS)
                 for_tile(u_squares, step - U_BIAS)
                 for_block(u_stats, step - U_STATS)
-                for_tile(w_affine, step - W_AFFINE)
+                for_tile(w_gain, step - W_GAIN)
+                for_tile(w_shift, step - W_SHIFT)
                 for_tile(w_squares, step - W_BIAS)
                 for_block(w_stats, step - W_STATS)
                 for_block(q_quantise, step - Q_QUANTISE)
                 for_block(j1_group, step - J1_GROUP)
                 for_block(j1_quantise, step - J1_QUANTISE)
+                for_block(u_rstd, step - U_RSTD)
+                for_block(w_rstd, step - W_RSTD)
                 for_block(o_store, step - O_STORE)
                 for_block(load, step - LOAD, ahead=3)

@@ -22,6 +22,7 @@ TILES = 4
 BLOCK = TILES * P
 BLOCKS = ROWS // BLOCK
 PASSES = D // (P * PACK)
+CLOCK_PASSES = 2
 
 FLOPS = 2 * ROWS * (D * D2 + D2 * D4)
 
@@ -99,6 +100,17 @@ def tile_multiheadedattention_pa_t_kernel(tc, query, A1W, A1b, g1, b1, A2W, A2b,
 
         def u_matmul(b, j):
             mm1 = psum.tile([P, D2], F32, name="mm1")
+            for extra in range(CLOCK_PASSES):
+                cols = slice(j * PASSES * P, (j * PASSES + 1) * P)
+                nc.tensor.matmul_mx(
+                    out=mm1[:],
+                    lhsT=held["q_codes", b][:, cols].bitcast(FP8X4),
+                    lhsT_scale=held["q_scales", b][:, cols],
+                    rhs=a1_codes[:, 0, :].bitcast(FP8X4),
+                    rhs_scale=a1_scales[:, 0, :],
+                    start=True,
+                    stop=True,
+                )
             for g in range(PASSES):
                 cols = slice((j * PASSES + g) * P, (j * PASSES + g + 1) * P)
                 nc.tensor.matmul_mx(
@@ -294,21 +306,6 @@ def tile_multiheadedattention_pa_t_kernel(tc, query, A1W, A1b, g1, b1, A2W, A2b,
         eps = const.tile([P, 1], F32)
         nc.vector.memset(eps[:], EPS)
 
-        a1_raw = const.tile([P, PASSES * PACK, D2], BF16)
-        nc.scalar.dma_start(
-            out=a1_raw[:].rearrange("p (h e) n -> p h (e n)", e=2),
-            in_=A1W.rearrange("(h p e) n -> p h (e n)", p=P, e=2),
-        )
-        a1_codes = const.tile([P, PASSES, D2], U32, align_bytes=64)
-        a1_scales = const.tile([P, PASSES, D2], U8, align_bytes=64)
-        for g in range(PASSES):
-            quantise_weight(
-                nc, const, a1_raw[:, g * PACK : (g + 1) * PACK, :], a1_codes[:, g, :], a1_scales[:, g, :], D2
-            )
-
-        a1b_all = const.tile([P, D2], BF16)
-        nc.scalar.dma_start(out=a1b_all[:], in_=A1b.partition_broadcast(P))
-
         gb_rows = const.tile([P, P], BF16)
         nc.vector.memset(gb_rows[:], 0.0)
         nc.scalar.dma_start(out=gb_rows[0:PACK, :], in_=g1.rearrange("(t p) -> t p", p=P))
@@ -319,6 +316,21 @@ def tile_multiheadedattention_pa_t_kernel(tc, query, A1W, A1b, g1, b1, A2W, A2b,
         nc.tensor.transpose(gb_ps[:, 0:P], gb_f32[:], ident[:])
         gb_cols = const.tile([P, 2 * PACK], F32)
         nc.vector.tensor_copy(out=gb_cols[:], in_=gb_ps[:, 0 : 2 * PACK])
+
+        a1_raw = const.tile([P, PASSES * PACK, D2], BF16)
+        a1_codes = const.tile([P, PASSES, D2], U32, align_bytes=64)
+        a1_scales = const.tile([P, PASSES, D2], U8, align_bytes=64)
+        for g in range(PASSES):
+            nc.scalar.dma_start(
+                out=a1_raw[:, g * PACK : (g + 1) * PACK, :].rearrange("p (u e) n -> p u (e n)", e=2),
+                in_=A1W[g * P * PACK : (g + 1) * P * PACK, :].rearrange("(u p e) n -> p u (e n)", p=P, e=2),
+            )
+            quantise_weight(
+                nc, const, a1_raw[:, g * PACK : (g + 1) * PACK, :], a1_codes[:, g, :], a1_scales[:, g, :], D2
+            )
+
+        a1b_all = const.tile([P, D2], BF16)
+        nc.scalar.dma_start(out=a1b_all[:], in_=A1b.partition_broadcast(P))
 
         a2_raw = const.tile([P, PACK, D4], BF16)
         nc.scalar.dma_start(out=a2_raw[:], in_=A2W.rearrange("(t p) n -> p t n", p=P))

@@ -22,7 +22,6 @@ TILES = 4
 BLOCK = TILES * P
 BLOCKS = ROWS // BLOCK
 PASSES = D // (P * PACK)
-CLOCK_PASSES = 2
 
 FLOPS = 2 * ROWS * (D * D2 + D2 * D4)
 
@@ -100,17 +99,6 @@ def tile_multiheadedattention_pa_t_kernel(tc, query, A1W, A1b, g1, b1, A2W, A2b,
 
         def u_matmul(b, j):
             mm1 = psum.tile([P, D2], F32, name="mm1")
-            for extra in range(CLOCK_PASSES):
-                cols = slice(j * PASSES * P, (j * PASSES + 1) * P)
-                nc.tensor.matmul_mx(
-                    out=mm1[:],
-                    lhsT=held["q_codes", b][:, cols].bitcast(FP8X4),
-                    lhsT_scale=held["q_scales", b][:, cols],
-                    rhs=a1_codes[:, 0, :].bitcast(FP8X4),
-                    rhs_scale=a1_scales[:, 0, :],
-                    start=True,
-                    stop=True,
-                )
             for g in range(PASSES):
                 cols = slice((j * PASSES + g) * P, (j * PASSES + g + 1) * P)
                 nc.tensor.matmul_mx(
@@ -297,7 +285,7 @@ def tile_multiheadedattention_pa_t_kernel(tc, query, A1W, A1b, g1, b1, A2W, A2b,
 
         def o_store(b):
             o_sb = held["o", b]
-            nc.scalar.activation(out=o_sb[:], in_=o_sb[:], func=ACT.Relu)
+            nc.vector.tensor_scalar_max(out=o_sb[:], in0=o_sb[:], scalar1=0.0)
             nc.sync.dma_start(out=out_rows[block_rows(b), :].rearrange("(p j) n -> p j n", j=TILES), in_=o_sb[:])
 
         load(0)

from contextlib import ExitStack

import concourse.mybir as mybir
from concourse.masks import make_identity

F32 = mybir.dt.float32
BF16 = mybir.dt.bfloat16
U32 = mybir.dt.uint32
U8 = mybir.dt.uint8
FP8X4 = mybir.dt.float8_e4m3fn_x4
ALU = mybir.AluOpType
ACT = mybir.ActivationFunctionType

P = 128
PACK = 4
ROWS = 512 * 17
D = 1024
D2 = 512
D4 = 256
EPS = 1e-5
TILES = 4
BLOCK = TILES * P
BLOCKS = ROWS // BLOCK
PASSES = D // (P * PACK)

FLOPS = 2 * ROWS * (D * D2 + D2 * D4)

Q_COPY = 0
LOAD = 3
Q_QUANTISE = 4
U_BIAS = 6
U_STATS = 10
U_RSTD = 11
U_NORMALISE = 12
J1_PLANE = 17
J1_GROUP = 22
J1_QUANTISE = 23
W_BIAS = 25
W_STATS = 29
W_RSTD = 30
W_GAIN = 30
W_SHIFT = 31
O_STORE = 35


def quantise_weight(nc, pool, raw, codes, scales, width):
    grouped = pool.tile([P, width, PACK], BF16, align_bytes=64, name="grouped", tag="grouped%d" % width)
    nc.vector.tensor_copy(out=grouped[:], in_=raw.rearrange("p t n -> p n t"))
    nc.vector.quantize_mx(
        out=codes.bitcast(FP8X4), scales=scales, in_=grouped[:].rearrange("p n t -> p (n t)")
    )


def tile_multiheadedattention_pa_t_kernel(tc, query, A1W, A1b, g1, b1, A2W, A2b, g2, b2, out):
    nc = tc.nc
    q_rows = query.flatten_outer_dims()
    out_rows = out.flatten_outer_dims()

    with ExitStack() as ctx:
        const = ctx.enter_context(tc.tile_pool(name="const", bufs=1))
        two = ctx.enter_context(tc.tile_pool(name="two", bufs=2))
        three = ctx.enter_context(tc.tile_pool(name="three", bufs=3))
        small = ctx.enter_context(tc.tile_pool(name="small", bufs=4))
        psum = ctx.enter_context(tc.psum_pool(name="psum", bufs=2))

        held = {}

        def block_rows(b):
            return slice(b * BLOCK, (b + 1) * BLOCK)

        def load(b):
            q_sb = three.tile([P, TILES * D], BF16, name="q_sb")
            nc.sync.dma_start(out=q_sb[:], in_=q_rows[block_rows(b), :].rearrange("(p j) k -> p (j k)", j=TILES))
            held["q_sb", b] = q_sb

        def q_transpose(b, j):
            q_words = held["q_sb", b][:].bitcast(F32)
            qT = psum.tile([P, D2], F32, name="qT")
            for h in range(D2 // P):
                col = j * D2 + h * P
                nc.tensor.transpose(qT[:, h * P : (h + 1) * P], q_words[:, col : col + P], ident[:])
            held["qT", b, j] = qT

        def q_copy(b, j):
            if j == 0:
                held["qg", b] = two.tile([P, TILES * D], BF16, align_bytes=64, name="qg")
            qg_words = held["qg", b][:].bitcast(F32)
            nc.scalar.copy(
                out=qg_words[:, j * D2 : (j + 1) * D2].rearrange("p (g r u) -> p g r u", g=PASSES, u=2),
                in_=held["qT", b, j][:].rearrange("p (g u r) -> p g r u", g=PASSES, u=2),
            )

        def q_quantise(b):
            q_codes = two.tile([P, TILES * PASSES * P], U32, align_bytes=64, name="q_codes")
            q_scales = two.tile([P, TILES * PASSES * P], U8, align_bytes=64, name="q_scales")
            nc.vector.quantize_mx(out=q_codes[:].bitcast(FP8X4), scales=q_scales[:], in_=held["qg", b][:])
            held["q_codes", b] = q_codes
            held["q_scales", b] = q_scales

        def u_matmul(b, j):
            mm1 = psum.tile([P, D2], F32, name="mm1")
            for g in range(PASSES):
                cols = slice((j * PASSES + g) * P, (j * PASSES + g + 1) * P)
                nc.tensor.matmul_mx(
                    out=mm1[:],
                    lhsT=held["q_codes", b][:, cols].bitcast(FP8X4),
                    lhsT_scale=held["q_scales", b][:, cols],
                    rhs=a1_codes[:, g, :].bitcast(FP8X4),
                    rhs_scale=a1_scales[:, g, :],
                    start=(g == 0),
                    stop=(g == PASSES - 1),
                )
            held["mm1", b, j] = mm1

        def u_bias(b, j):
            if j == 0:
                held["u", b] = three.tile([P, TILES, D2], F32, name="u_sb")
                held["u_sum", b] = small.tile([P, TILES], F32, name="u_sum")
            nc.vector.scalar_tensor_tensor(
                out=held["u", b][:, j, :],
                in0=held["mm1", b, j][:],
                scalar=1.0,
                in1=a1b_all[:],
                op0=ALU.mult,
                op1=ALU.add,
                accum_out=held["u_sum", b][:, j : j + 1],
            )

        def u_squares(b, j):
            if j == 0:
                held["u_sq", b] = two.tile([P, TILES, D2], BF16, name="u_sq")
                held["u_ssq", b] = small.tile([P, TILES], F32, name="u_ssq")
            nc.scalar.activation(
                out=held["u_sq", b][:, j, :],
                in_=held["u", b][:, j, :],
                func=ACT.Square,
                bias=held["u_sum", b][:, j : j + 1],
                scale=-1.0 * D2,
                accum_out=held["u_ssq", b][:, j : j + 1],
            )

        def u_stats(b):
            u_std = small.tile([P, TILES], F32, name="u_std")
            nc.scalar.activation(
                out=u_std[:], in_=held["u_ssq", b][:], func=ACT.Sqrt, bias=eps[:, 0:1], scale=1.0 / (D2 * D2 * D2)
            )
            u_negmean = small.tile([P, TILES], F32, name="u_negmean")
            nc.gpsimd.tensor_scalar(
                out=u_negmean[:], in0=held["u_sum", b][:], scalar1=-1.0 / D2, scalar2=0.0, op0=ALU.mult, op1=ALU.add
            )
            held["u_std", b] = u_std
            held["u_negmean", b] = u_negmean

        def u_rstd(b):
            held["u_rstd", b] = small.tile([P, TILES], F32, name="u_rstd")
            nc.vector.reciprocal(out=held["u_rstd", b][:], in_=held["u_std", b][:])

        def u_normalise(b, j):
            if j == 0:
                held["y", b] = two.tile([P, TILES, D2], F32, name="y_sb")
            nc.vector.tensor_scalar(
                out=held["y", b][:, j, :],
                in0=held["u", b][:, j, :],
                scalar1=held["u_negmean", b][:, j : j + 1],
                scalar2=held["u_rstd", b][:, j : j + 1],
                op0=ALU.add,
                op1=ALU.mult,
            )

        def y_transpose(b, t):
            yT = psum.tile([P, BLOCK], F32, name="yT")
            for j in range(TILES):
                nc.tensor.transpose(yT[:, j * P : (j + 1) * P], held["y", b][:, j, t * P : (t + 1) * P], ident[:])
            held["yT", b, t] = yT

        def j1_plane(b, t):
            if t == 0:
                held["j1_planes", b] = two.tile([P, PACK, BLOCK], BF16, name="j1_planes")
            nc.scalar.activation(
                out=held["j1_planes", b][:, t, :],
                in_=held["yT", b, t][:],
                func=ACT.Relu,
                bias=gb_cols[:, PACK + t : PACK + t + 1],
                scale=gb_cols[:, t : t + 1],
            )

        def j1_group(b):
            j1_grouped = two.tile([P, BLOCK, PACK], BF16, align_bytes=64, name="j1_grouped")
            nc.vector.tensor_copy(
                out=j1_grouped[:].rearrange("p (c i) t -> p c t i", i=4),
                in_=held["j1_planes", b][:].rearrange("p t (c i) -> p c t i", i=4),
            )
            held["j1_grouped", b] = j1_grouped

        def j1_quantise(b):
            j1_codes = two.tile([P, BLOCK], U32, align_bytes=64, name="j1_codes")
            j1_scales = two.tile([P, BLOCK], U8, align_bytes=64, name="j1_scales")
            nc.vector.quantize_mx(
                out=j1_codes[:].bitcast(FP8X4),
                scales=j1_scales[:],
                in_=held["j1_grouped", b][:].rearrange("p r t -> p (r t)"),
            )
            held["j1_codes", b] = j1_codes
            held["j1_scales", b] = j1_scales

        def w_matmul(b, j):
            mm2 = psum.tile([P, D4], F32, name="mm2")
            nc.tensor.matmul_mx(
                out=mm2[:],
                lhsT=held["j1_codes", b][:, j * P : (j + 1) * P].bitcast(FP8X4),
                lhsT_scale=held["j1_scales", b][:, j * P : (j + 1) * P],
                rhs=a2_codes[:].bitcast(FP8X4),
                rhs_scale=a2_scales[:],
                start=True,
                stop=True,
            )
            held["mm2", b, j] = mm2

        def w_bias(b, j):
            if j == 0:
                held["w", b] = three.tile([P, TILES, D4], F32, name="w_sb")
                held["w_sum", b] = small.tile([P, TILES], F32, name="w_sum")
            nc.vector.scalar_tensor_tensor(
                out=held["w", b][:, j, :],
                in0=held["mm2", b, j][:],
                scalar=1.0,
                in1=a2b_all[:],
                op0=ALU.mult,
                op1=ALU.add,
                accum_out=held["w_sum", b][:, j : j + 1],
            )

        def w_squares(b, j):
            if j == 0:
                held["w_sq", b] = two.tile([P, TILES, D4], BF16, name="w_sq")
                held["w_ssq", b] = small.tile([P, TILES], F32, name="w_ssq")
            nc.scalar.activation(
                out=held["w_sq", b][:, j, :],
                in_=held["w", b][:, j, :],
                func=ACT.Square,
                bias=held["w_sum", b][:, j : j + 1],
                scale=-1.0 * D4,
                accum_out=held["w_ssq", b][:, j : j + 1],
            )

        def w_stats(b):
            w_std = small.tile([P, TILES], F32, name="w_std")
            nc.scalar.activation(
                out=w_std[:], in_=held["w_ssq", b][:], func=ACT.Sqrt, bias=eps[:, 0:1], scale=1.0 / (D4 * D4 * D4)
            )
            w_negmean = small.tile([P, TILES], F32, name="w_negmean")
            nc.gpsimd.tensor_scalar(
                out=w_negmean[:], in0=held["w_sum", b][:], scalar1=-1.0 / D4, scalar2=0.0, op0=ALU.mult, op1=ALU.add
            )
            held["w_std", b] = w_std
            held["w_negmean", b] = w_negmean

        def w_rstd(b):
            held["w_rstd", b] = small.tile([P, TILES], F32, name="w_rstd")
            nc.vector.reciprocal(out=held["w_rstd", b][:], in_=held["w_std", b][:])

        def w_gain(b, j):
            if j == 0:
                held["w_gain", b] = two.tile([P, TILES, D4], F32, name="w_gain")
            nc.vector.scalar_tensor_tensor(
                out=held["w_gain", b][:, j, :],
                in0=held["w", b][:, j, :],
                scalar=held["w_negmean", b][:, j : j + 1],
                in1=g2_all[:],
                op0=ALU.add,
                op1=ALU.mult,
            )

        def w_shift(b, j):
            if j == 0:
                held["o", b] = three.tile([P, TILES, D4], F32, name="o_sb")
            nc.vector.scalar_tensor_tensor(
                out=held["o", b][:, j, :],
                in0=held["w_gain", b][:, j, :],
                scalar=held["w_rstd", b][:, j : j + 1],
                in1=b2_all[:],
                op0=ALU.mult,
                op1=ALU.add,
            )

        def o_store(b):
            o_sb = held["o", b]
            nc.vector.tensor_scalar_max(out=o_sb[:], in0=o_sb[:], scalar1=0.0)
            nc.sync.dma_start(out=out_rows[block_rows(b), :].rearrange("(p j) n -> p j n", j=TILES), in_=o_sb[:])

        load(0)
        ident = const.tile([P, P], F32)
        make_identity(nc, ident[:])
        eps = const.tile([P, 1], F32)
        nc.vector.memset(eps[:], EPS)

        gb_rows = const.tile([P, P], BF16)
        nc.vector.memset(gb_rows[:], 0.0)
        nc.scalar.dma_start(out=gb_rows[0:PACK, :], in_=g1.rearrange("(t p) -> t p", p=P))
        nc.scalar.dma_start(out=gb_rows[PACK : 2 * PACK, :], in_=b1.rearrange("(t p) -> t p", p=P))
        gb_f32 = const.tile([P, P], F32)
        nc.vector.tensor_copy(out=gb_f32[:], in_=gb_rows[:])
        gb_ps = psum.tile([P, BLOCK], F32, name="yT")
        nc.tensor.transpose(gb_ps[:, 0:P], gb_f32[:], ident[:])
        gb_cols = const.tile([P, 2 * PACK], F32)
        nc.vector.tensor_copy(out=gb_cols[:], in_=gb_ps[:, 0 : 2 * PACK])

        a1_raw = const.tile([P, PASSES * PACK, D2], BF16)
        a1_codes = const.tile([P, PASSES, D2], U32, align_bytes=64)
        a1_scales = const.tile([P, PASSES, D2], U8, align_bytes=64)
        for g in range(PASSES):
            nc.scalar.dma_start(
                out=a1_raw[:, g * PACK : (g + 1) * PACK, :].rearrange("p (u e) n -> p u (e n)", e=2),
                in_=A1W[g * P * PACK : (g + 1) * P * PACK, :].rearrange("(u p e) n -> p u (e n)", p=P, e=2),
            )
            quantise_weight(
                nc, const, a1_raw[:, g * PACK : (g + 1) * PACK, :], a1_codes[:, g, :], a1_scales[:, g, :], D2
            )

        a1b_all = const.tile([P, D2], BF16)
        nc.scalar.dma_start(out=a1b_all[:], in_=A1b.partition_broadcast(P))

        a2_raw = const.tile([P, PACK, D4], BF16)
        nc.scalar.dma_start(out=a2_raw[:], in_=A2W.rearrange("(t p) n -> p t n", p=P))
        a2_codes = const.tile([P, D4], U32, align_bytes=64)
        a2_scales = const.tile([P, D4], U8, align_bytes=64)
        quantise_weight(nc, const, a2_raw[:], a2_codes[:], a2_scales[:], D4)
        a2b_all = const.tile([P, D4], BF16)
        nc.scalar.dma_start(out=a2b_all[:], in_=A2b.partition_broadcast(P))
        g2_all = const.tile([P, D4], BF16)
        nc.scalar.dma_start(out=g2_all[:], in_=g2.partition_broadcast(P))
        b2_all = const.tile([P, D4], BF16)
        nc.scalar.dma_start(out=b2_all[:], in_=b2.partition_broadcast(P))

        load(1)
        load(2)

        def for_tile(stage, n):
            if 0 <= n < BLOCKS * TILES:
                stage(n // TILES, n % TILES)

        def for_block(stage, n, ahead=0):
            if n % TILES == 0 and 0 <= n // TILES + ahead < BLOCKS and n >= 0:
                stage(n // TILES + ahead)

        with tc.manual_schedule():
            for step in range(-1, BLOCKS * TILES + O_STORE + 1):
                for_tile(q_transpose, step + 1 - Q_COPY)
                for_tile(y_transpose, step + 1 - J1_PLANE)
                for_tile(u_matmul, step + 1 - U_BIAS)
                for_tile(w_matmul, step + 1 - W_BIAS)

                for_tile(u_bias, step - U_BIAS)
                for_tile(q_copy, step - Q_COPY)
                for_tile(u_normalise, step - U_NORMALISE)
                for_tile(j1_plane, step - J1_PLANE)
                for_tile(w_bias, step - W_BIAS)
                for_tile(u_squares, step - U_BIAS)
                for_block(u_stats, step - U_STATS)
                for_tile(w_gain, step - W_GAIN)
                for_tile(w_shift, step - W_SHIFT)
                for_tile(w_squares, step - W_BIAS)
                for_block(w_stats, step - W_STATS)
                for_block(q_quantise, step - Q_QUANTISE)
                for_block(j1_group, step - J1_GROUP)
                for_block(j1_quantise, step - J1_QUANTISE)
                for_block(u_rstd, step - U_RSTD)
                for_block(w_rstd, step - W_RSTD)
                for_block(o_store, step - O_STORE)
                for_block(load, step - LOAD, ahead=3)
